import numpy as np
import ml_dtypes


def mxq(x, axis, fmt="e4m3"):
    dtype, down = {"e4m3": (ml_dtypes.float8_e4m3fn, 7), "e5m2": (ml_dtypes.float8_e5m2, 14)}[fmt]
    v = np.moveaxis(np.asarray(x, np.float32).astype(ml_dtypes.bfloat16).astype(np.float64), axis, -1)
    blocks = v.reshape(v.shape[:-1] + (-1, 32))
    amax = np.abs(blocks).max(-1, keepdims=True)
    byte = np.maximum(np.where(amax > 0, np.frexp(amax)[1] - 1 + 127, 0) - down, 1)
    scale = np.exp2(byte - 127.0)
    codes = (blocks / scale).astype(np.float32).astype(dtype).astype(np.float64)
    return np.moveaxis((codes * scale).reshape(v.shape), -1, axis)


WIDE = False


def mx_kscale(k):
    if not WIDE:
        return np.ones(k)
    levels = np.array([10, -10, 5, -5, 0])
    a = np.random.permutation(np.resize(levels, k // 512 * 4)).reshape(k // 512, 4)
    idx = np.arange(k)
    return np.exp2(a[idx // 512, idx % 128 // 32])


BF16 = ml_dtypes.bfloat16


def bf(x):
    return np.asarray(x, np.float32).astype(BF16)


def f64(x):
    return np.asarray(x).astype(np.float64)


B, F, O = 8192, 1024, 128


def setup_inputs():
    s = mx_kscale(F)
    return {"x": bf(np.random.standard_normal((B, 2, F)) * s),
            "filters_real": bf(np.random.standard_normal((O, F)) * 0.5 / np.sqrt(F) / s),
            "filters_imag": bf(np.random.standard_normal((O, F)) * 0.5 / np.sqrt(F) / s)}


def reference(x, filters_real, filters_imag):
    x = f64(x)
    x_real = x[:, 0]
    x_imag = x[:, 1]
    w_r = f64(filters_real) + f64(filters_imag)
    w_i = f64(filters_real) - f64(filters_imag)
    energies = (mxq(x_real, 1, "e4m3") @ mxq(w_r, 1, "e4m3").T) + (mxq(x_imag, 1, "e4m3") @ mxq(w_i, 1, "e4m3").T)
    return energies

@@ -1,0 +1,164 @@
+from contextlib import ExitStack
+
+import concourse.mybir as mybir
+from concourse.masks import make_identity
+
+FLOPS = 2 * 8192 * 2048 * 128
+
+F32 = mybir.dt.float32
+BF16 = mybir.dt.bfloat16
+U32 = mybir.dt.uint32
+U8 = mybir.dt.uint8
+FP8X4 = mybir.dt.float8_e4m3fn_x4
+ADD = mybir.AluOpType.add
+SUB = mybir.AluOpType.subtract
+
+P = 128
+K = 2048
+PASSES = 4
+GROUP_TILES = [1, 1, 2] + [4] * 14 + [2, 1, 1]
+X_BUFS = 8
+PIN = True
+RUN = 2
+
+
+def tile_fftmlp_t_kernel(tc, x, filters_real, filters_imag, out):
+    nc = tc.nc
+    n_groups = len(GROUP_TILES)
+    bases = [P * sum(GROUP_TILES[:gi]) for gi in range(n_groups)]
+    row_tiles = [(gi, t) for gi in range(n_groups) for t in range(GROUP_TILES[gi])]
+    n_rt = len(row_tiles)
+    assert n_rt * P == x.shape[0]
+
+    with ExitStack() as ctx:
+        consts = ctx.enter_context(tc.tile_pool(name="consts", bufs=1))
+        xpool = ctx.enter_context(tc.tile_pool(name="xpool", bufs=X_BUFS))
+        gpool = ctx.enter_context(tc.tile_pool(name="gpool", bufs=4))
+        qpool = ctx.enter_context(tc.tile_pool(name="qpool", bufs=6))
+        opool = ctx.enter_context(tc.tile_pool(name="opool", bufs=3))
+        psum_t = ctx.enter_context(tc.psum_pool(name="psum_t", bufs=6))
+        psum_o = ctx.enter_context(tc.psum_pool(name="psum_o", bufs=2))
+        if PIN:
+            ctx.enter_context(tc.manual_schedule())
+
+        x_tiles = {}
+        banks = {}
+        grouped = {}
+        codes = {}
+        scales = {}
+        o_banks = {}
+
+        def load(gi):
+            n_t = GROUP_TILES[gi]
+            x_sb = xpool.tile([P, n_t * K], BF16, tag="x", name="x_sb")
+            rows = x[bases[gi] : bases[gi] + P * n_t]
+            nc.sync.dma_start(out=x_sb[:], in_=rows.rearrange("(p t) c f -> p (t c f)", t=n_t))
+            x_tiles[gi] = x_sb
+
+        def transposes(r):
+            gi, t = row_tiles[r]
+            words = x_tiles[gi][:].bitcast(F32)
+            for h in range(2):
+                bank = psum_t.tile([P, 4, P], F32, tag="xt", name="bank")
+                for j in range(4):
+                    w0 = t * (K // 2) + (4 * h + j) * P
+                    nc.tensor.transpose(bank[:, j, :], words[:, w0 : w0 + P], ident_f32[:])
+                banks[(r, h)] = bank
+
+        def copy_out(r, h, on_vector):
+            if h == 0:
+                grouped[r] = gpool.tile([P, 4 * PASSES * P], BF16, tag="grouped", name="grouped", align_bytes=64)
+            dst = grouped[r][:].bitcast(F32).rearrange("p (g r u) -> p g r u", g=PASSES, u=2)
+            src = banks[(r, h)][:].rearrange("p (g u) r -> p g r u", u=2)
+            if on_vector:
+                nc.vector.tensor_copy(out=dst[:, 2 * h : 2 * h + 2], in_=src)
+            else:
+                nc.scalar.copy(out=dst[:, 2 * h : 2 * h + 2], in_=src)
+
+        def quantise(r):
+            codes[r] = qpool.tile([P, PASSES * P], U32, tag="codes", name="codes", align_bytes=64)
+            scales[r] = qpool.tile([P, PASSES * P], U8, tag="scales", name="scales", align_bytes=64)
+            nc.vector.quantize_mx(out=codes[r][:].bitcast(FP8X4), scales=scales[r][:], in_=grouped[r][:])
+
+        def multiply(r):
+            gi, t = row_tiles[r]
+            if t == 0:
+                o_banks[gi] = psum_o.tile([P, 4 * P], F32, tag="o", name="o_bank")
+            for g in range(PASSES):
+                cols = slice(g * P, (g + 1) * P)
+                nc.tensor.matmul_mx(
+                    out=o_banks[gi][:, t * P : (t + 1) * P],
+                    lhsT=codes[r][:, cols].bitcast(FP8X4),
+                    lhsT_scale=scales[r][:, cols],
+                    rhs=w_codes[:, cols].bitcast(FP8X4),
+                    rhs_scale=w_scales[:, cols],
+                    start=(g == 0),
+                    stop=(g == PASSES - 1),
+                )
+            if t == GROUP_TILES[gi] - 1:
+                n_t = GROUP_TILES[gi]
+                o_sb = opool.tile([P, 4 * P], F32, tag="o_sb", name="o_sb")
+                nc.scalar.copy(out=o_sb[:, : n_t * P], in_=o_banks[gi][:, : n_t * P])
+                rows = out[bases[gi] : bases[gi] + P * n_t, :]
+                nc.sync.dma_start(out=rows.rearrange("(p t) o -> p (t o)", t=n_t), in_=o_sb[:, : n_t * P])
+
+        fr = consts.tile([P, 1024], BF16, name="fr")
+        fi = consts.tile([P, 1024], BF16, name="fi")
+        nc.sync.dma_start(out=fr[:], in_=filters_real)
+        nc.sync.dma_start(out=fi[:], in_=filters_imag)
+        for gi in range(X_BUFS):
+            load(gi)
+        loaded = [X_BUFS]
+
+        ident_f32 = consts.tile([P, P], F32, name="ident_f32")
+        make_identity(nc, ident_f32[:])
+        ident_bf = consts.tile([P, P], BF16, name="ident_bf")
+        make_identity(nc, ident_bf[:])
+
+        w_perm = consts.tile([P, 2, 8, P], BF16, name="w_perm")
+        for c, op in ((0, ADD), (1, SUB)):
+            nc.vector.tensor_tensor(
+                out=w_perm[:, c].rearrange("o (a e) p -> o a e p", e=2),
+                in0=fr[:].rearrange("o (a p e) -> o a e p", a=4, e=2),
+                in1=fi[:].rearrange("o (a p e) -> o a e p", a=4, e=2),
+                op=op,
+            )
+        w_grouped = consts.tile([P, 4 * PASSES * P], BF16, name="w_grouped", align_bytes=64)
+        w_codes = consts.tile([P, PASSES * P], U32, name="w_codes", align_bytes=64)
+        w_scales = consts.tile([P, PASSES * P], U8, name="w_scales", align_bytes=64)
+
+        def weights():
+            w_dst = w_grouped[:].rearrange("p (g o t) -> p g o t", g=PASSES, t=4)
+            for c in range(2):
+                w_bank = psum_t.tile([P, 8, P], BF16, tag="xt", name="w_bank")
+                for j in range(8):
+                    nc.tensor.transpose(w_bank[:, j, :], w_perm[:, c, j, :], ident_bf[:])
+                w_src = w_bank[:].rearrange("p (g t) o -> p g o t", t=4)
+                if c == 0:
+                    nc.scalar.copy(out=w_dst[:, 0:2], in_=w_src)
+                else:
+                    nc.vector.tensor_copy(out=w_dst[:, 2:4], in_=w_src)
+            nc.vector.quantize_mx(out=w_codes[:].bitcast(FP8X4), scales=w_scales[:], in_=w_grouped[:])
+
+        n_steps = n_rt // RUN
+        for b in range(n_steps + 1):
+            run = list(range(b * RUN, (b + 1) * RUN)) if b < n_steps else []
+            for r in run:
+                transposes(r)
+                gi, t = row_tiles[r]
+                if t == GROUP_TILES[gi] - 1 and loaded[0] < n_groups:
+                    load(loaded[0])
+                    loaded[0] += 1
+            if b > 0 and (b * RUN - 1) not in codes:
+                quantise(b * RUN - 1)
+            for r in run:
+                copy_out(r, 0, False)
+                vec = (r % 2 == 0) or (r == n_rt - 1)
+                copy_out(r, 1, vec)
+                if vec:
+                    quantise(r)
+            if b == 0:
+                weights()
+            if b > 0:
+                for r in range((b - 1) * RUN, b * RUN):
+                    multiply(r)

@@ -35,7 +35,7 @@ def tile_fftmlp_t_kernel(tc, x, filters_real, filters_imag, out):
         xpool = ctx.enter_context(tc.tile_pool(name="xpool", bufs=X_BUFS))
         gpool = ctx.enter_context(tc.tile_pool(name="gpool", bufs=4))
         qpool = ctx.enter_context(tc.tile_pool(name="qpool", bufs=6))
-        opool = ctx.enter_context(tc.tile_pool(name="opool", bufs=3))
+        opool = ctx.enter_context(tc.tile_pool(name="opool", bufs=len(GROUP_TILES)))
         psum_t = ctx.enter_context(tc.psum_pool(name="psum_t", bufs=6))
         psum_o = ctx.enter_context(tc.psum_pool(name="psum_o", bufs=2))
         if PIN:

@@ -17,9 +17,11 @@ P = 128
 K = 2048
 PASSES = 4
 GROUP_TILES = [1, 1, 2] + [4] * 14 + [2, 1, 1]
-X_BUFS = 8
+X_BUFS = 7
 PIN = True
-RUN = 2
+T_BANKS = 6
+O_BANKS = 2
+RUNS = [[0, 1], [2, 3]] + [list(range(r, r + 4)) for r in range(4, 60, 4)] + [[60, 61], [62, 63]]
 
 
 def tile_fftmlp_t_kernel(tc, x, filters_real, filters_imag, out):
@@ -33,11 +35,11 @@ def tile_fftmlp_t_kernel(tc, x, filters_real, filters_imag, out):
     with ExitStack() as ctx:
         consts = ctx.enter_context(tc.tile_pool(name="consts", bufs=1))
         xpool = ctx.enter_context(tc.tile_pool(name="xpool", bufs=X_BUFS))
-        gpool = ctx.enter_context(tc.tile_pool(name="gpool", bufs=4))
-        qpool = ctx.enter_context(tc.tile_pool(name="qpool", bufs=6))
+        gpool = ctx.enter_context(tc.tile_pool(name="gpool", bufs=6))
+        qpool = ctx.enter_context(tc.tile_pool(name="qpool", bufs=10))
         opool = ctx.enter_context(tc.tile_pool(name="opool", bufs=len(GROUP_TILES)))
-        psum_t = ctx.enter_context(tc.psum_pool(name="psum_t", bufs=6))
-        psum_o = ctx.enter_context(tc.psum_pool(name="psum_o", bufs=2))
+        psum_t = ctx.enter_context(tc.psum_pool(name="psum_t", bufs=T_BANKS))
+        psum_o = ctx.enter_context(tc.psum_pool(name="psum_o", bufs=O_BANKS))
         if PIN:
             ctx.enter_context(tc.manual_schedule())
 
@@ -140,25 +142,26 @@ def tile_fftmlp_t_kernel(tc, x, filters_real, filters_imag, out):
                     nc.vector.tensor_copy(out=w_dst[:, 2:4], in_=w_src)
             nc.vector.quantize_mx(out=w_codes[:].bitcast(FP8X4), scales=w_scales[:], in_=w_grouped[:])
 
-        n_steps = n_rt // RUN
-        for b in range(n_steps + 1):
-            run = list(range(b * RUN, (b + 1) * RUN)) if b < n_steps else []
-            for r in run:
+        for b in range(len(RUNS) + 1):
+            run = RUNS[b] if b < len(RUNS) else []
+            done = 0
+            for i, r in enumerate(run):
                 transposes(r)
                 gi, t = row_tiles[r]
                 if t == GROUP_TILES[gi] - 1 and loaded[0] < n_groups:
                     load(loaded[0])
                     loaded[0] += 1
-            if b > 0 and (b * RUN - 1) not in codes:
-                quantise(b * RUN - 1)
-            for r in run:
                 copy_out(r, 0, False)
-                vec = (r % 2 == 0) or (r == n_rt - 1)
-                copy_out(r, 1, vec)
-                if vec:
-                    quantise(r)
+                if (i % 2 == 0) or (r == n_rt - 1):
+                    copy_out(r, 1, True)
+                    quantise(run[done])
+                    done += 1
+                else:
+                    copy_out(r, 1, False)
+            for i in range(done, len(run)):
+                quantise(run[i])
             if b == 0:
                 weights()
             if b > 0:
-                for r in range((b - 1) * RUN, b * RUN):
+                for r in RUNS[b - 1]:
                     multiply(r)

from contextlib import ExitStack

import concourse.mybir as mybir
from concourse.masks import make_identity

FLOPS = 2 * 8192 * 2048 * 128

F32 = mybir.dt.float32
BF16 = mybir.dt.bfloat16
U32 = mybir.dt.uint32
U8 = mybir.dt.uint8
FP8X4 = mybir.dt.float8_e4m3fn_x4
ADD = mybir.AluOpType.add
SUB = mybir.AluOpType.subtract

P = 128
K = 2048
PASSES = 4
GROUP_TILES = [1, 1, 2] + [4] * 14 + [2, 1, 1]
X_BUFS = 7
PIN = True
T_BANKS = 6
O_BANKS = 2
RUNS = [[0, 1], [2, 3]] + [list(range(r, r + 4)) for r in range(4, 60, 4)] + [[60, 61], [62, 63]]


def tile_fftmlp_t_kernel(tc, x, filters_real, filters_imag, out):
    nc = tc.nc
    n_groups = len(GROUP_TILES)
    bases = [P * sum(GROUP_TILES[:gi]) for gi in range(n_groups)]
    row_tiles = [(gi, t) for gi in range(n_groups) for t in range(GROUP_TILES[gi])]
    n_rt = len(row_tiles)
    assert n_rt * P == x.shape[0]

    with ExitStack() as ctx:
        consts = ctx.enter_context(tc.tile_pool(name="consts", bufs=1))
        xpool = ctx.enter_context(tc.tile_pool(name="xpool", bufs=X_BUFS))
        gpool = ctx.enter_context(tc.tile_pool(name="gpool", bufs=6))
        qpool = ctx.enter_context(tc.tile_pool(name="qpool", bufs=10))
        opool = ctx.enter_context(tc.tile_pool(name="opool", bufs=len(GROUP_TILES)))
        psum_t = ctx.enter_context(tc.psum_pool(name="psum_t", bufs=T_BANKS))
        psum_o = ctx.enter_context(tc.psum_pool(name="psum_o", bufs=O_BANKS))
        if PIN:
            ctx.enter_context(tc.manual_schedule())

        x_tiles = {}
        banks = {}
        grouped = {}
        codes = {}
        scales = {}
        o_banks = {}

        def load(gi):
            n_t = GROUP_TILES[gi]
            x_sb = xpool.tile([P, n_t * K], BF16, tag="x", name="x_sb")
            rows = x[bases[gi] : bases[gi] + P * n_t]
            nc.sync.dma_start(out=x_sb[:], in_=rows.rearrange("(p t) c f -> p (t c f)", t=n_t))
            x_tiles[gi] = x_sb

        def transposes(r):
            gi, t = row_tiles[r]
            words = x_tiles[gi][:].bitcast(F32)
            for h in range(2):
                bank = psum_t.tile([P, 4, P], F32, tag="xt", name="bank")
                for j in range(4):
                    w0 = t * (K // 2) + (4 * h + j) * P
                    nc.tensor.transpose(bank[:, j, :], words[:, w0 : w0 + P], ident_f32[:])
                banks[(r, h)] = bank

        def copy_out(r, h, on_vector):
            if h == 0:
                grouped[r] = gpool.tile([P, 4 * PASSES * P], BF16, tag="grouped", name="grouped", align_bytes=64)
            dst = grouped[r][:].bitcast(F32).rearrange("p (g r u) -> p g r u", g=PASSES, u=2)
            src = banks[(r, h)][:].rearrange("p (g u) r -> p g r u", u=2)
            if on_vector:
                nc.vector.tensor_copy(out=dst[:, 2 * h : 2 * h + 2], in_=src)
            else:
                nc.scalar.copy(out=dst[:, 2 * h : 2 * h + 2], in_=src)

        def quantise(r):
            codes[r] = qpool.tile([P, PASSES * P], U32, tag="codes", name="codes", align_bytes=64)
            scales[r] = qpool.tile([P, PASSES * P], U8, tag="scales", name="scales", align_bytes=64)
            nc.vector.quantize_mx(out=codes[r][:].bitcast(FP8X4), scales=scales[r][:], in_=grouped[r][:])

        def multiply(r):
            gi, t = row_tiles[r]
            if t == 0:
                o_banks[gi] = psum_o.tile([P, 4 * P], F32, tag="o", name="o_bank")
            for g in range(PASSES):
                cols = slice(g * P, (g + 1) * P)
                nc.tensor.matmul_mx(
                    out=o_banks[gi][:, t * P : (t + 1) * P],
                    lhsT=codes[r][:, cols].bitcast(FP8X4),
                    lhsT_scale=scales[r][:, cols],
                    rhs=w_codes[:, cols].bitcast(FP8X4),
                    rhs_scale=w_scales[:, cols],
                    start=(g == 0),
                    stop=(g == PASSES - 1),
                )
            if t == GROUP_TILES[gi] - 1:
                n_t = GROUP_TILES[gi]
                o_sb = opool.tile([P, 4 * P], F32, tag="o_sb", name="o_sb")
                nc.scalar.copy(out=o_sb[:, : n_t * P], in_=o_banks[gi][:, : n_t * P])
                rows = out[bases[gi] : bases[gi] + P * n_t, :]
                nc.sync.dma_start(out=rows.rearrange("(p t) o -> p (t o)", t=n_t), in_=o_sb[:, : n_t * P])

        fr = consts.tile([P, 1024], BF16, name="fr")
        fi = consts.tile([P, 1024], BF16, name="fi")
        nc.sync.dma_start(out=fr[:], in_=filters_real)
        nc.sync.dma_start(out=fi[:], in_=filters_imag)
        for gi in range(X_BUFS):
            load(gi)
        loaded = [X_BUFS]

        ident_f32 = consts.tile([P, P], F32, name="ident_f32")
        make_identity(nc, ident_f32[:])
        ident_bf = consts.tile([P, P], BF16, name="ident_bf")
        make_identity(nc, ident_bf[:])

        w_perm = consts.tile([P, 2, 8, P], BF16, name="w_perm")
        for c, op in ((0, ADD), (1, SUB)):
            nc.vector.tensor_tensor(
                out=w_perm[:, c].rearrange("o (a e) p -> o a e p", e=2),
                in0=fr[:].rearrange("o (a p e) -> o a e p", a=4, e=2),
                in1=fi[:].rearrange("o (a p e) -> o a e p", a=4, e=2),
                op=op,
            )
        w_grouped = consts.tile([P, 4 * PASSES * P], BF16, name="w_grouped", align_bytes=64)
        w_codes = consts.tile([P, PASSES * P], U32, name="w_codes", align_bytes=64)
        w_scales = consts.tile([P, PASSES * P], U8, name="w_scales", align_bytes=64)

        def weights():
            w_dst = w_grouped[:].rearrange("p (g o t) -> p g o t", g=PASSES, t=4)
            for c in range(2):
                w_bank = psum_t.tile([P, 8, P], BF16, tag="xt", name="w_bank")
                for j in range(8):
                    nc.tensor.transpose(w_bank[:, j, :], w_perm[:, c, j, :], ident_bf[:])
                w_src = w_bank[:].rearrange("p (g t) o -> p g o t", t=4)
                if c == 0:
                    nc.scalar.copy(out=w_dst[:, 0:2], in_=w_src)
                else:
                    nc.vector.tensor_copy(out=w_dst[:, 2:4], in_=w_src)
            nc.vector.quantize_mx(out=w_codes[:].bitcast(FP8X4), scales=w_scales[:], in_=w_grouped[:])

        for b in range(len(RUNS) + 1):
            run = RUNS[b] if b < len(RUNS) else []
            done = 0
            for i, r in enumerate(run):
                transposes(r)
                gi, t = row_tiles[r]
                if t == GROUP_TILES[gi] - 1 and loaded[0] < n_groups:
                    load(loaded[0])
                    loaded[0] += 1
                copy_out(r, 0, False)
                if (i % 2 == 0) or (r == n_rt - 1):
                    copy_out(r, 1, True)
                    quantise(run[done])
                    done += 1
                else:
                    copy_out(r, 1, False)
            for i in range(done, len(run)):
                quantise(run[i])
            if b == 0:
                weights()
            if b > 0:
                for r in RUNS[b - 1]:
                    multiply(r)
